import numpy as np
import ml_dtypes


def mxq(x, axis, fmt="e4m3"):
    dtype, down = {"e4m3": (ml_dtypes.float8_e4m3fn, 7), "e5m2": (ml_dtypes.float8_e5m2, 14)}[fmt]
    v = np.moveaxis(np.asarray(x, np.float32).astype(ml_dtypes.bfloat16).astype(np.float64), axis, -1)
    blocks = v.reshape(v.shape[:-1] + (-1, 32))
    amax = np.abs(blocks).max(-1, keepdims=True)
    byte = np.maximum(np.where(amax > 0, np.frexp(amax)[1] - 1 + 127, 0) - down, 1)
    scale = np.exp2(byte - 127.0)
    codes = (blocks / scale).astype(np.float32).astype(dtype).astype(np.float64)
    return np.moveaxis((codes * scale).reshape(v.shape), -1, axis)


WIDE = False


def mx_kscale(k):
    if not WIDE:
        return np.ones(k)
    levels = np.array([10, -10, 5, -5, 0])
    if k % 512:
        return np.exp2(np.random.permutation(np.resize(levels, k // 32))).repeat(32)
    a = np.empty((k // 512, 16))
    for p in range(k // 512):
        a[p, :8] = np.random.permutation(np.resize(levels, 8))
        for g in range(8):
            far = levels[np.abs(levels - a[p, g]) >= 10]
            a[p, g + 8] = far[np.random.randint(len(far))]
    return np.exp2(a.ravel()).repeat(32)


BF16 = ml_dtypes.bfloat16


def bf(x):
    return np.asarray(x, np.float32).astype(BF16)


def f64(x):
    return np.asarray(x).astype(np.float64)


C, P, B, D = 7, 512, 2, 256
N = C * P
ID = C // 2


def laplacian_with_self_loop(adj):
    a = adj + np.eye(adj.shape[0])
    d_inv_sqrt = 1.0 / np.sqrt(a.sum(axis=1))
    return d_inv_sqrt[:, None] * a * d_inv_sqrt[None, :]


def setup_inputs():
    s = mx_kscale(P)
    sp = s / s.min()
    r = np.exp2(np.random.uniform(-1.0, 1.0, N))
    adj = np.random.uniform(0.0, 1.0, (N, N)) * r[:, None] * np.tile(sp, C)[None, :]
    x = np.random.standard_normal((P, B * D)) * (0.15 * N * sp.mean() / np.sqrt(P / 3.0)) / sp[:, None]
    return {"globalAdj": bf(adj), "inputs": bf(x), "batch_size": B, "output_dim": D, "id": ID}


def reference(globalAdj, inputs, batch_size, output_dim, id):
    lap = laplacian_with_self_loop(f64(globalAdj))
    col = lap[:, id * P:(id + 1) * P]
    out = mxq(col, 1, "e4m3") @ mxq(f64(inputs), 0, "e4m3")
    out = out.reshape(N, batch_size, output_dim)
    return out.transpose(1, 0, 2)

@@ -1,0 +1,238 @@
+from contextlib import ExitStack
+
+import concourse.mybir as mybir
+from concourse.masks import make_identity
+
+FLOPS = 2 * 3584 * 512 * 512
+
+BF16 = mybir.dt.bfloat16
+F32 = mybir.dt.float32
+U32 = mybir.dt.uint32
+U8 = mybir.dt.uint8
+FP8X4 = mybir.dt.float8_e4m3fn_x4
+ALU = mybir.AluOpType
+ACT = mybir.ActivationFunctionType
+
+P = 128
+N = 3584
+K = 512
+CS = 2048
+A_BUFS = 7
+TAIL_V = 3
+
+
+def tile_gcn_kernel(tc, adj, feats, batch_size, output_dim, client, out):
+    nc = tc.nc
+    col0 = client * K
+    units = [(col0, 4), (0, 4), (512, 4), (1024, 4), (2048, 4), (2560, 4), (3072, 2), (3328, 1), (3456, 1)]
+    pieces = []
+    for u, (base, rows) in enumerate(units):
+        for r0 in range(0, rows, 2):
+            pieces.append((u, r0, min(2, rows - r0)))
+    n = len(pieces)
+
+    with ExitStack() as ctx:
+        const = ctx.enter_context(tc.tile_pool(name="const", bufs=1))
+        apool = ctx.enter_context(tc.tile_pool(name="apool", bufs=A_BUFS))
+        junk = ctx.enter_context(tc.tile_pool(name="junk", bufs=2))
+        work = ctx.enter_context(tc.tile_pool(name="work", bufs=3))
+        small = ctx.enter_context(tc.tile_pool(name="small", bufs=5))
+        ypool = ctx.enter_context(tc.tile_pool(name="ypool", bufs=1))
+        ps_t = ctx.enter_context(tc.psum_pool(name="ps_t", bufs=3))
+        ps_y = ctx.enter_context(tc.psum_pool(name="ps_y", bufs=4))
+        ps_d = ctx.enter_context(tc.psum_pool(name="ps_d", bufs=1))
+        ctx.enter_context(tc.manual_schedule())
+
+        a_t, s_v, s_s, dinv = {}, {}, {}, {}
+        plus, colb, xt, grp, codes, scl, y_ps, y_sb = {}, {}, {}, {}, {}, {}, {}, {}
+
+        ident_b = const.tile([P, P], BF16, name="ident_b")
+        ident_f = const.tile([P, P], F32, name="ident_f")
+        epad = const.tile([P, K + 4], BF16, name="epad")
+        x_raw = const.tile([P, 4, K], BF16, name="x_raw")
+        x_grp = const.tile([P, K, 4], BF16, name="x_grp", align_bytes=64)
+        x_codes = const.tile([P, K], U32, name="x_codes", align_bytes=64)
+        x_scales = const.tile([P, K], U8, name="x_scales", align_bytes=64)
+        djb = const.tile([P, P, 4], F32, name="djb")
+        dj_flat = djb[:].rearrange("m n r -> m (n r)")
+
+        def load(k):
+            u, r0, nr = pieces[k]
+            base, rows = units[u]
+            a_t[k] = apool.tile([P, 2, N], BF16, name="a_t")
+            src = adj[base : base + P * rows, :].rearrange("(p r) c -> p r c", r=rows)
+            if u == 0:
+                for j in range(nr):
+                    nc.sync.dma_start(out=a_t[k][:, j : j + 1, :], in_=src[:, r0 + j : r0 + j + 1, :])
+            else:
+                nc.sync.dma_start(out=a_t[k][:, 0:nr, :], in_=src[:, r0 : r0 + nr, :])
+
+        def sums(k):
+            u, r0, nr = pieces[k]
+            s_v[k] = small.tile([P, 2], F32, name="s_v")
+            s_s[k] = small.tile([P, 2], F32, name="s_s")
+            for j in range(nr):
+                half = (N - j * CS) // 2
+                junk_v = junk.tile([P, N // 2], F32, name="junk_v")
+                nc.vector.scalar_tensor_tensor(
+                    out=junk_v[:, 0:half],
+                    in0=a_t[k][:, j, 0:half],
+                    scalar=1.0,
+                    in1=a_t[k][:, j, half : 2 * half],
+                    op0=ALU.mult,
+                    op1=ALU.add,
+                    accum_out=s_v[k][:, j : j + 1],
+                )
+            if nr == 2:
+                junk_s = junk.tile([P, CS], BF16, name="junk_s")
+                nc.scalar.activation(
+                    out=junk_s[:],
+                    in_=a_t[k][:, 1, N - CS : N],
+                    func=ACT.Copy,
+                    bias=1.0 / CS,
+                    accum_out=s_s[k][:, 0:1],
+                )
+
+        def add_identity(k):
+            u, r0, nr = pieces[k]
+            plus[k] = const.tile([P, 2, K], F32, name="plus%d" % k)
+            for j in range(nr):
+                r = r0 + j
+                nc.vector.tensor_tensor(
+                    out=plus[k][:, j, :],
+                    in0=a_t[k][:, j, col0 : col0 + K],
+                    in1=epad[:, 3 - r : 3 - r + K],
+                    op=ALU.add,
+                )
+
+        def rsqrt(k):
+            nr = pieces[k][2]
+            if pieces[k][0] == 0:
+                dinv[k] = dinv0[:, 2 * k : 2 * k + 2]
+            else:
+                dinv[k] = small.tile([P, 2], F32, name="dinv")
+            for j in range(nr):
+                nc.scalar.activation(
+                    out=dinv[k][:, j : j + 1],
+                    in_=s_v[k][:, j : j + 1],
+                    func=ACT.Abs_reciprocal_sqrt,
+                    bias=(1.0 if j == 0 else s_s[k][:, 0:1]),
+                )
+
+        def scale_transpose(k):
+            u, r0, nr = pieces[k]
+            colb[k] = work.tile([P, 2, K], BF16, name="colb")
+            xt[k] = ps_t.tile([P, 2, 2, P], F32, name="xt")
+            for j in range(nr):
+                blk = plus[k][:, j, :] if u == 0 else a_t[k][:, j, col0 : col0 + K]
+                nc.vector.scalar_tensor_tensor(
+                    out=colb[k][:, j, :],
+                    in0=blk,
+                    scalar=dinv[k][:, j : j + 1],
+                    in1=dj_flat,
+                    op0=ALU.mult,
+                    op1=ALU.mult,
+                )
+                words = colb[k][:, j, :].bitcast(F32)
+                for w in range(2):
+                    nc.tensor.transpose(xt[k][:, j, w, :], words[:, w : K // 2 : 2], ident_f[:])
+
+        def regroup(k):
+            nr = pieces[k][2]
+            grp[k] = work.tile([P, 2, P, 4], BF16, name="grp", align_bytes=64)
+            nc.scalar.copy(
+                out=grp[k][:, 0:nr, :, :].bitcast(F32), in_=xt[k][:, 0:nr, :, :].rearrange("q r w i -> q r i w")
+            )
+
+        def quant_mm(k):
+            nr = pieces[k][2]
+            codes[k] = work.tile([P, 2 * P], U32, name="codes", align_bytes=64)
+            scl[k] = work.tile([P, 2 * P], U8, name="scl", align_bytes=64)
+            nc.vector.quantize_mx(
+                out=codes[k][:, 0 : nr * P].bitcast(FP8X4),
+                scales=scl[k][:, 0 : nr * P],
+                in_=grp[k][:, 0:nr, :, :].rearrange("q r i t -> q (r i t)"),
+            )
+            for j in range(nr):
+                y_ps[(k, j)] = ps_y.tile([P, K], F32, name="y_ps")
+                nc.tensor.matmul_mx(
+                    out=y_ps[(k, j)][:],
+                    lhsT=codes[k][:, j * P : (j + 1) * P].bitcast(FP8X4),
+                    lhsT_scale=scl[k][:, j * P : (j + 1) * P],
+                    rhs=x_codes[:].bitcast(FP8X4),
+                    rhs_scale=x_scales[:],
+                    start=True,
+                    stop=True,
+                )
+
+        def leave(k):
+            u, r0, nr = pieces[k]
+            base, rows = units[u]
+            if r0 == 0:
+                y_sb[u] = ypool.tile([P, 2, rows, 256], F32, name="y_sb%d" % u)
+            for j in range(nr):
+                dst = y_sb[u][:, :, r0 + j, :]
+                src = y_ps[(k, j)][:].rearrange("p (b f) -> p b f", b=2)
+                if k >= n - TAIL_V and (k + j) % 2 == 1:
+                    nc.vector.tensor_copy(out=dst, in_=src)
+                else:
+                    nc.scalar.copy(out=dst, in_=src)
+            if r0 + nr == rows:
+                nc.sync.dma_start(
+                    out=out[:, base : base + P * rows, :].rearrange("b (p r) f -> p b (r f)", r=rows),
+                    in_=y_sb[u][:].rearrange("p b r f -> p b (r f)"),
+                )
+
+        load(0)
+        load(1)
+        nc.sync.dma_start(out=x_raw[:], in_=feats.rearrange("(q t) f -> q t f", t=4))
+        for k in range(2, A_BUFS):
+            load(k)
+        make_identity(nc, ident_b[:])
+        nc.gpsimd.memset(epad[:], 0.0)
+        nc.gpsimd.tensor_copy(
+            out=epad[:, 3 : 3 + K].rearrange("p (q r) -> p q r", r=4)[:, :, 0], in_=ident_b[:]
+        )
+        make_identity(nc, ident_f[:])
+        warm = const.tile([P, 1], F32, name="warm")
+        nc.vector.memset(warm[:], 1.0)
+        nc.scalar.activation(out=warm[:], in_=warm[:], func=ACT.Abs_reciprocal_sqrt)
+        dinv0 = const.tile([P, 4], F32, name="dinv0")
+
+        for k in range(2):
+            sums(k)
+            rsqrt(k)
+        dj_ps = ps_d.tile([P, 4, P], F32, name="dj_ps")
+        for r in range(4):
+            nc.tensor.matmul(
+                out=dj_ps[:, r, :],
+                lhsT=dinv0[:, r : r + 1].to_broadcast([P, P]),
+                rhs=ident_f[:],
+                start=True,
+                stop=True,
+            )
+        nc.scalar.copy(out=x_grp[:], in_=x_raw[:].rearrange("q t f -> q f t"))
+        add_identity(0)
+        add_identity(1)
+        nc.vector.tensor_copy(out=djb[:], in_=dj_ps[:].rearrange("m r n -> m n r"))
+        scale_transpose(0)
+        load(A_BUFS)
+        nc.vector.quantize_mx(
+            out=x_codes[:].bitcast(FP8X4), scales=x_scales[:], in_=x_grp[:].rearrange("q f t -> q (f t)")
+        )
+
+        for k in range(2, n + 3):
+            if k < n:
+                sums(k)
+            if k - 2 < n:
+                regroup(k - 2)
+            if k < n:
+                rsqrt(k)
+            if k - 1 < n:
+                scale_transpose(k - 1)
+                if k - 1 + A_BUFS < n:
+                    load(k - 1 + A_BUFS)
+            if k - 2 < n:
+                quant_mm(k - 2)
+            if k >= 3:
+                leave(k - 3)

@@ -16,7 +16,7 @@ ACT = mybir.ActivationFunctionType
 P = 128
 N = 3584
 K = 512
-CS = 2048
+CS = 2432
 A_BUFS = 7
 TAIL_V = 3
 

@@ -16,35 +16,33 @@ ACT = mybir.ActivationFunctionType
 P = 128
 N = 3584
 K = 512
-CS = 2432
-A_BUFS = 7
-TAIL_V = 3
+CS = 1152
+R = 3
+T = (N - K) // (P * R)
+ROWWISE = 8
+A_BUFS = 5
+LAST = T - 1
 
 
 def tile_gcn_kernel(tc, adj, feats, batch_size, output_dim, client, out):
     nc = tc.nc
     col0 = client * K
-    units = [(col0, 4), (0, 4), (512, 4), (1024, 4), (2048, 4), (2560, 4), (3072, 2), (3328, 1), (3456, 1)]
-    pieces = []
-    for u, (base, rows) in enumerate(units):
-        for r0 in range(0, rows, 2):
-            pieces.append((u, r0, min(2, rows - r0)))
-    n = len(pieces)
+    base = [P * R * t + (K if P * R * t >= col0 else 0) for t in range(T)]
 
     with ExitStack() as ctx:
         const = ctx.enter_context(tc.tile_pool(name="const", bufs=1))
         apool = ctx.enter_context(tc.tile_pool(name="apool", bufs=A_BUFS))
         junk = ctx.enter_context(tc.tile_pool(name="junk", bufs=2))
-        work = ctx.enter_context(tc.tile_pool(name="work", bufs=3))
-        small = ctx.enter_context(tc.tile_pool(name="small", bufs=5))
+        junk1 = ctx.enter_context(tc.tile_pool(name="junk1", bufs=1))
+        work = ctx.enter_context(tc.tile_pool(name="work", bufs=4))
+        small = ctx.enter_context(tc.tile_pool(name="small", bufs=4))
         ypool = ctx.enter_context(tc.tile_pool(name="ypool", bufs=1))
-        ps_t = ctx.enter_context(tc.psum_pool(name="ps_t", bufs=3))
+        ps_t = ctx.enter_context(tc.psum_pool(name="ps_t", bufs=4))
         ps_y = ctx.enter_context(tc.psum_pool(name="ps_y", bufs=4))
-        ps_d = ctx.enter_context(tc.psum_pool(name="ps_d", bufs=1))
         ctx.enter_context(tc.manual_schedule())
 
-        a_t, s_v, s_s, dinv = {}, {}, {}, {}
-        plus, colb, xt, grp, codes, scl, y_ps, y_sb = {}, {}, {}, {}, {}, {}, {}, {}
+        a_row, d, dinv, blk = {}, {}, {}, {}
+        colb, xt, grp, codes, scl, y_ps, y_sb = {}, {}, {}, {}, {}, {}, {}
 
         ident_b = const.tile([P, P], BF16, name="ident_b")
         ident_f = const.tile([P, P], F32, name="ident_f")
@@ -55,155 +53,142 @@ def tile_gcn_kernel(tc, adj, feats, batch_size, output_dim, client, out):
         x_scales = const.tile([P, K], U8, name="x_scales", align_bytes=64)
         djb = const.tile([P, P, 4], F32, name="djb")
         dj_flat = djb[:].rearrange("m n r -> m (n r)")
+        s_v = const.tile([P, 4], F32, name="s_v")
+        s_s = const.tile([P, 4], F32, name="s_s")
+        dinv0 = const.tile([P, 4], F32, name="dinv0")
+        warm = const.tile([P, 1], F32, name="warm")
 
-        def load(k):
-            u, r0, nr = pieces[k]
-            base, rows = units[u]
-            a_t[k] = apool.tile([P, 2, N], BF16, name="a_t")
-            src = adj[base : base + P * rows, :].rearrange("(p r) c -> p r c", r=rows)
-            if u == 0:
-                for j in range(nr):
-                    nc.sync.dma_start(out=a_t[k][:, j : j + 1, :], in_=src[:, r0 + j : r0 + j + 1, :])
+        def load_client(lo, hi):
+            for t0 in range(lo, hi):
+                if t0 % R == 0:
+                    a_row["tile"] = apool.tile([P, R, N], BF16, name="a_t")
+                a_row[t0] = a_row["tile"][:, t0 % R, :]
+                src = adj[col0 : col0 + K, :].rearrange("(p r) c -> p r c", r=4)
+                nc.sync.dma_start(out=a_row["tile"][:, t0 % R : t0 % R + 1, :], in_=src[:, t0 : t0 + 1, :])
+
+        def load(t):
+            a_t = apool.tile([P, R, N], BF16, name="a_t")
+            src = adj[base[t] : base[t] + P * R, :].rearrange("(p r) c -> p r c", r=R)
+            if t < ROWWISE:
+                for j in range(R):
+                    nc.sync.dma_start(out=a_t[:, j : j + 1, :], in_=src[:, j : j + 1, :])
             else:
-                nc.sync.dma_start(out=a_t[k][:, 0:nr, :], in_=src[:, r0 : r0 + nr, :])
+                nc.sync.dma_start(out=a_t[:], in_=src)
+            for j in range(R):
+                a_row[4 + R * t + j] = a_t[:, j, :]
 
-        def sums(k):
-            u, r0, nr = pieces[k]
-            s_v[k] = small.tile([P, 2], F32, name="s_v")
-            s_s[k] = small.tile([P, 2], F32, name="s_s")
-            for j in range(nr):
-                half = (N - j * CS) // 2
-                junk_v = junk.tile([P, N // 2], F32, name="junk_v")
-                nc.vector.scalar_tensor_tensor(
-                    out=junk_v[:, 0:half],
-                    in0=a_t[k][:, j, 0:half],
-                    scalar=1.0,
-                    in1=a_t[k][:, j, half : 2 * half],
-                    op0=ALU.mult,
-                    op1=ALU.add,
-                    accum_out=s_v[k][:, j : j + 1],
-                )
-            if nr == 2:
-                junk_s = junk.tile([P, CS], BF16, name="junk_s")
-                nc.scalar.activation(
-                    out=junk_s[:],
-                    in_=a_t[k][:, 1, N - CS : N],
-                    func=ACT.Copy,
-                    bias=1.0 / CS,
-                    accum_out=s_s[k][:, 0:1],
-                )
-
-        def add_identity(k):
-            u, r0, nr = pieces[k]
-            plus[k] = const.tile([P, 2, K], F32, name="plus%d" % k)
-            for j in range(nr):
-                r = r0 + j
-                nc.vector.tensor_tensor(
-                    out=plus[k][:, j, :],
-                    in0=a_t[k][:, j, col0 : col0 + K],
-                    in1=epad[:, 3 - r : 3 - r + K],
-                    op=ALU.add,
-                )
-
-        def rsqrt(k):
-            nr = pieces[k][2]
-            if pieces[k][0] == 0:
-                dinv[k] = dinv0[:, 2 * k : 2 * k + 2]
-            else:
-                dinv[k] = small.tile([P, 2], F32, name="dinv")
-            for j in range(nr):
-                nc.scalar.activation(
-                    out=dinv[k][:, j : j + 1],
-                    in_=s_v[k][:, j : j + 1],
-                    func=ACT.Abs_reciprocal_sqrt,
-                    bias=(1.0 if j == 0 else s_s[k][:, 0:1]),
-                )
-
-        def scale_transpose(k):
-            u, r0, nr = pieces[k]
-            colb[k] = work.tile([P, 2, K], BF16, name="colb")
-            xt[k] = ps_t.tile([P, 2, 2, P], F32, name="xt")
-            for j in range(nr):
-                blk = plus[k][:, j, :] if u == 0 else a_t[k][:, j, col0 : col0 + K]
-                nc.vector.scalar_tensor_tensor(
-                    out=colb[k][:, j, :],
-                    in0=blk,
-                    scalar=dinv[k][:, j : j + 1],
-                    in1=dj_flat,
-                    op0=ALU.mult,
-                    op1=ALU.mult,
-                )
-                words = colb[k][:, j, :].bitcast(F32)
-                for w in range(2):
-                    nc.tensor.transpose(xt[k][:, j, w, :], words[:, w : K // 2 : 2], ident_f[:])
-
-        def regroup(k):
-            nr = pieces[k][2]
-            grp[k] = work.tile([P, 2, P, 4], BF16, name="grp", align_bytes=64)
-            nc.scalar.copy(
-                out=grp[k][:, 0:nr, :, :].bitcast(F32), in_=xt[k][:, 0:nr, :, :].rearrange("q r w i -> q r i w")
+        def sum_vector(n, cols, acc):
+            half = cols // 2
+            junk_v = junk.tile([P, N // 2], BF16, name="junk_v")
+            nc.vector.scalar_tensor_tensor(
+                out=junk_v[:, 0:half],
+                in0=a_row[n][:, 0:half],
+                scalar=1.0,
+                in1=a_row[n][:, half : 2 * half],
+                op0=ALU.mult,
+                op1=ALU.add,
+                accum_out=acc,
             )
 
-        def quant_mm(k):
-            nr = pieces[k][2]
-            codes[k] = work.tile([P, 2 * P], U32, name="codes", align_bytes=64)
-            scl[k] = work.tile([P, 2 * P], U8, name="scl", align_bytes=64)
+        def sum_scalar(n, cols, acc, bias):
+            junk_s = junk1.tile([P, N], BF16, name="junk_s")
+            nc.scalar.activation(
+                out=junk_s[:, 0:cols], in_=a_row[n][:, N - cols : N], func=ACT.Copy, bias=bias, accum_out=acc
+            )
+
+        def client_row(r):
+            sum_vector(r, N - CS, s_v[:, r : r + 1])
+            sum_scalar(r, CS, s_s[:, r : r + 1], 1.0 / CS)
+            nc.scalar.activation(
+                out=dinv0[:, r : r + 1], in_=s_v[:, r : r + 1], func=ACT.Abs_reciprocal_sqrt, bias=s_s[:, r : r + 1]
+            )
+            dinv[r] = dinv0[:, r : r + 1]
+            plus = const.tile([P, K], F32, name="plus%d" % r)
+            nc.vector.tensor_tensor(
+                out=plus[:], in0=a_row[r][:, col0 : col0 + K], in1=epad[:, 3 - r : 3 - r + K], op=ALU.add
+            )
+            blk[r] = plus[:]
+
+        def sums_scalar(t):
+            d[t] = small.tile([P, R], F32, name="d")
+            sum_scalar(4 + R * t, N, d[t][:, 0:1], 0.0)
+
+        def sums_vector(t, j):
+            sum_vector(4 + R * t + j, N, d[t][:, j : j + 1])
+
+        def rsqrt(t):
+            di = small.tile([P, R], F32, name="di")
+            nc.scalar.activation(out=di[:], in_=d[t][:], func=ACT.Abs_reciprocal_sqrt, bias=1.0)
+            for j in range(R):
+                dinv[4 + R * t + j] = di[:, j : j + 1]
+                blk[4 + R * t + j] = a_row[4 + R * t + j][:, col0 : col0 + K]
+
+        def scale(n):
+            q, j = divmod(n, 2)
+            colb = work.tile([P, K], BF16, name="colb")
+            if j == 0:
+                xt[q] = ps_t.tile([P, 2, 2, P], F32, name="xt")
+            nc.vector.scalar_tensor_tensor(
+                out=colb[:], in0=blk[n], scalar=dinv[n], in1=dj_flat, op0=ALU.mult, op1=ALU.mult
+            )
+            words = colb[:].bitcast(F32)
+            for w in range(2):
+                nc.tensor.transpose(xt[q][:, j, w, :], words[:, w : K // 2 : 2], ident_f[:])
+
+        def regroup(q):
+            grp[q] = work.tile([P, 2, P, 4], BF16, name="grp", align_bytes=64)
+            nc.scalar.copy(out=grp[q][:].bitcast(F32), in_=xt[q][:].rearrange("q r w i -> q r i w"))
+
+        def quant_mm(q):
+            codes[q] = work.tile([P, 2 * P], U32, name="codes", align_bytes=64)
+            scl[q] = work.tile([P, 2 * P], U8, name="scl", align_bytes=64)
             nc.vector.quantize_mx(
-                out=codes[k][:, 0 : nr * P].bitcast(FP8X4),
-                scales=scl[k][:, 0 : nr * P],
-                in_=grp[k][:, 0:nr, :, :].rearrange("q r i t -> q (r i t)"),
+                out=codes[q][:].bitcast(FP8X4), scales=scl[q][:], in_=grp[q][:].rearrange("q r i t -> q (r i t)")
             )
-            for j in range(nr):
-                y_ps[(k, j)] = ps_y.tile([P, K], F32, name="y_ps")
+            for j in range(2):
+                y_ps[2 * q + j] = ps_y.tile([P, K], F32, name="y_ps")
                 nc.tensor.matmul_mx(
-                    out=y_ps[(k, j)][:],
-                    lhsT=codes[k][:, j * P : (j + 1) * P].bitcast(FP8X4),
-                    lhsT_scale=scl[k][:, j * P : (j + 1) * P],
+                    out=y_ps[2 * q + j][:],
+                    lhsT=codes[q][:, j * P : (j + 1) * P].bitcast(FP8X4),
+                    lhsT_scale=scl[q][:, j * P : (j + 1) * P],
                     rhs=x_codes[:].bitcast(FP8X4),
                     rhs_scale=x_scales[:],
                     start=True,
                     stop=True,
                 )
 
-        def leave(k):
-            u, r0, nr = pieces[k]
-            base, rows = units[u]
-            if r0 == 0:
-                y_sb[u] = ypool.tile([P, 2, rows, 256], F32, name="y_sb%d" % u)
-            for j in range(nr):
-                dst = y_sb[u][:, :, r0 + j, :]
-                src = y_ps[(k, j)][:].rearrange("p (b f) -> p b f", b=2)
-                if k >= n - TAIL_V and (k + j) % 2 == 1:
-                    nc.vector.tensor_copy(out=dst, in_=src)
-                else:
-                    nc.scalar.copy(out=dst, in_=src)
-            if r0 + nr == rows:
-                nc.sync.dma_start(
-                    out=out[:, base : base + P * rows, :].rearrange("b (p r) f -> p b (r f)", r=rows),
-                    in_=y_sb[u][:].rearrange("p b r f -> p b (r f)"),
-                )
+        def leave(n, engine):
+            t, j = (-1, n) if n < 4 else divmod(n - 4, R)
+            rows = 4 if t < 0 else R
+            if j == 0:
+                y_sb[t] = ypool.tile([P, 2, rows, 256], F32, name="y_sb%d" % (t + 1))
+            engine(out=y_sb[t][:, :, j, :], in_=y_ps[n][:].rearrange("p (b f) -> p b f", b=2))
+            first = col0 if t < 0 else base[t]
+            dst = out[:, first : first + P * rows, :].rearrange("b (p r) f -> p b r f", r=rows)
+            if t == LAST:
+                stores.append((dst[:, :, j, :], y_sb[t][:, :, j, :]))
+            elif j == rows - 1:
+                stores.append((
+                    out[:, first : first + P * rows, :].rearrange("b (p r) f -> p b (r f)", r=rows),
+                    y_sb[t][:].rearrange("p b r f -> p b (r f)"),
+                ))
 
-        load(0)
-        load(1)
+        load_client(0, 4)
         nc.sync.dma_start(out=x_raw[:], in_=feats.rearrange("(q t) f -> q t f", t=4))
-        for k in range(2, A_BUFS):
-            load(k)
+        for t in range(A_BUFS - 2):
+            load(t)
         make_identity(nc, ident_b[:])
         nc.gpsimd.memset(epad[:], 0.0)
         nc.gpsimd.tensor_copy(
             out=epad[:, 3 : 3 + K].rearrange("p (q r) -> p q r", r=4)[:, :, 0], in_=ident_b[:]
         )
         make_identity(nc, ident_f[:])
-        warm = const.tile([P, 1], F32, name="warm")
         nc.vector.memset(warm[:], 1.0)
         nc.scalar.activation(out=warm[:], in_=warm[:], func=ACT.Abs_reciprocal_sqrt)
-        dinv0 = const.tile([P, 4], F32, name="dinv0")
 
-        for k in range(2):
-            sums(k)
-            rsqrt(k)
-        dj_ps = ps_d.tile([P, 4, P], F32, name="dj_ps")
+        dj_ps = ps_t.tile([P, 4, P], F32, name="xt")
         for r in range(4):
+            client_row(r)
             nc.tensor.matmul(
                 out=dj_ps[:, r, :],
                 lhsT=dinv0[:, r : r + 1].to_broadcast([P, P]),
@@ -212,27 +197,78 @@ def tile_gcn_kernel(tc, adj, feats, batch_size, output_dim, client, out):
                 stop=True,
             )
         nc.scalar.copy(out=x_grp[:], in_=x_raw[:].rearrange("q t f -> q f t"))
-        add_identity(0)
-        add_identity(1)
         nc.vector.tensor_copy(out=djb[:], in_=dj_ps[:].rearrange("m r n -> m n r"))
-        scale_transpose(0)
-        load(A_BUFS)
+        for n in range(4):
+            scale(n)
         nc.vector.quantize_mx(
             out=x_codes[:].bitcast(FP8X4), scales=x_scales[:], in_=x_grp[:].rearrange("q f t -> q (f t)")
         )
 
-        for k in range(2, n + 3):
-            if k < n:
-                sums(k)
-            if k - 2 < n:
-                regroup(k - 2)
-            if k < n:
-                rsqrt(k)
-            if k - 1 < n:
-                scale_transpose(k - 1)
-                if k - 1 + A_BUFS < n:
-                    load(k - 1 + A_BUFS)
-            if k - 2 < n:
-                quant_mm(k - 2)
-            if k >= 3:
-                leave(k - 3)
+        stores = []
+        loaded = A_BUFS - 2
+        done = 4
+        quanted = 0
+        left = 0
+        for t in range(T - 1):
+            ready = range(quanted, done // 2)
+            if t >= 1:
+                rsqrt(t - 1)
+            for q in ready:
+                regroup(q)
+            sums_scalar(t)
+            sums_vector(t, 1)
+            if t >= 1:
+                scale(done)
+                scale(done + 1)
+            for q in ready:
+                quant_mm(q)
+            sums_vector(t, 2)
+            if t >= 1:
+                scale(done + 2)
+                done += 3
+            quanted = ready.stop
+            for step in range(2 if t == 0 else 1):
+                if loaded < T:
+                    load(loaded)
+                    loaded += 1
+            for n in range(left, 2 * quanted):
+                leave(n, nc.scalar.copy)
+            left = 2 * quanted
+            if loaded == T:
+                for dst, src in stores:
+                    nc.sync.dma_start(out=dst, in_=src)
+                stores = []
+        V, S = nc.vector.tensor_copy, nc.scalar.copy
+        rsqrt(T - 2)
+        regroup(9)
+        regroup(10)
+        sums_scalar(T - 1)
+        sums_vector(T - 1, 1)
+        quant_mm(9)
+        quant_mm(10)
+        sums_vector(T - 1, 2)
+        rsqrt(T - 1)
+        scale(22)
+        scale(23)
+        leave(18, S)
+        leave(19, S)
+        regroup(11)
+        scale(24)
+        scale(25)
+        leave(20, S)
+        leave(21, S)
+        quant_mm(11)
+        regroup(12)
+        scale(26)
+        scale(27)
+        leave(22, S)
+        quant_mm(12)
+        regroup(13)
+        leave(23, V)
+        leave(24, S)
+        quant_mm(13)
+        leave(25, V)
+        leave(26, S)
+        leave(27, V)
+        for dst, src in stores:
+            nc.sync.dma_start(out=dst, in_=src)

@@ -19,15 +19,20 @@ K = 512
 CS = 1152
 R = 3
 T = (N - K) // (P * R)
-ROWWISE = 8
-A_BUFS = 5
+UNITS = [(0, 12), (2048, 3), (2432, 3), (2816, 3), (3200, 3)]
+LUMPS = {t: [1, 1, 1] for t in range(8)}
+A_BUFS = 6
 LAST = T - 1
+CT = 1536
 
 
 def tile_gcn_kernel(tc, adj, feats, batch_size, output_dim, client, out):
     nc = tc.nc
     col0 = client * K
-    base = [P * R * t + (K if P * R * t >= col0 else 0) for t in range(T)]
+    place = []
+    for first, width in UNITS:
+        for r0 in range(0, width, R):
+            place.append((first, width, r0))
 
     with ExitStack() as ctx:
         const = ctx.enter_context(tc.tile_pool(name="const", bufs=1))
@@ -37,11 +42,12 @@ def tile_gcn_kernel(tc, adj, feats, batch_size, output_dim, client, out):
         work = ctx.enter_context(tc.tile_pool(name="work", bufs=4))
         small = ctx.enter_context(tc.tile_pool(name="small", bufs=4))
         ypool = ctx.enter_context(tc.tile_pool(name="ypool", bufs=1))
-        ps_t = ctx.enter_context(tc.psum_pool(name="ps_t", bufs=4))
+        ps_t = ctx.enter_context(tc.psum_pool(name="ps_t", bufs=3))
+        ps_d = ctx.enter_context(tc.psum_pool(name="ps_d", bufs=1))
         ps_y = ctx.enter_context(tc.psum_pool(name="ps_y", bufs=4))
         ctx.enter_context(tc.manual_schedule())
 
-        a_row, d, dinv, blk = {}, {}, {}, {}
+        a_row, d, pre, dinv, blk = {}, {}, {}, {}, {}
         colb, xt, grp, codes, scl, y_ps, y_sb = {}, {}, {}, {}, {}, {}, {}
 
         ident_b = const.tile([P, P], BF16, name="ident_b")
@@ -51,8 +57,8 @@ def tile_gcn_kernel(tc, adj, feats, batch_size, output_dim, client, out):
         x_grp = const.tile([P, K, 4], BF16, name="x_grp", align_bytes=64)
         x_codes = const.tile([P, K], U32, name="x_codes", align_bytes=64)
         x_scales = const.tile([P, K], U8, name="x_scales", align_bytes=64)
-        djb = const.tile([P, P, 4], F32, name="djb")
-        dj_flat = djb[:].rearrange("m n r -> m (n r)")
+        dj_ps = ps_d.tile([P, 4, P], F32, name="dj_ps")
+        dj_flat = dj_ps[:].rearrange("m r n -> m n r")
         s_v = const.tile([P, 4], F32, name="s_v")
         s_s = const.tile([P, 4], F32, name="s_s")
         dinv0 = const.tile([P, 4], F32, name="dinv0")
@@ -68,12 +74,12 @@ def tile_gcn_kernel(tc, adj, feats, batch_size, output_dim, client, out):
 
         def load(t):
             a_t = apool.tile([P, R, N], BF16, name="a_t")
-            src = adj[base[t] : base[t] + P * R, :].rearrange("(p r) c -> p r c", r=R)
-            if t < ROWWISE:
-                for j in range(R):
-                    nc.sync.dma_start(out=a_t[:, j : j + 1, :], in_=src[:, j : j + 1, :])
-            else:
-                nc.sync.dma_start(out=a_t[:], in_=src)
+            first, width, r0 = place[t]
+            src = adj[first : first + P * width, :].rearrange("(p r) c -> p r c", r=width)
+            j = 0
+            for rows in LUMPS.get(t, [R]):
+                nc.sync.dma_start(out=a_t[:, j : j + rows, :], in_=src[:, r0 + j : r0 + j + rows, :])
+                j += rows
             for j in range(R):
                 a_row[4 + R * t + j] = a_t[:, j, :]
 
@@ -85,6 +91,30 @@ def tile_gcn_kernel(tc, adj, feats, batch_size, output_dim, client, out):
                 in0=a_row[n][:, 0:half],
                 scalar=1.0,
                 in1=a_row[n][:, half : 2 * half],
+                op0=ALU.mult,
+                op1=ALU.add,
+                accum_out=acc,
+            )
+
+        def presum_tensor(n):
+            chunks = N // K - 1
+            pre[n] = ps_t.tile([P, K], F32, name="xt")
+            for c in range(chunks):
+                nc.tensor.matmul(
+                    out=pre[n][:],
+                    lhsT=ident_b[:],
+                    rhs=a_row[n][:, c * K : (c + 1) * K],
+                    start=c == 0,
+                    stop=c == chunks - 1,
+                )
+
+        def sum_presummed(n, acc):
+            junk_v = junk.tile([P, N // 2], BF16, name="junk_v")
+            nc.vector.scalar_tensor_tensor(
+                out=junk_v[:, 0:K],
+                in0=a_row[n][:, N - K : N],
+                scalar=1.0,
+                in1=pre[n][:],
                 op0=ALU.mult,
                 op1=ALU.add,
                 accum_out=acc,
@@ -123,13 +153,27 @@ def tile_gcn_kernel(tc, adj, feats, batch_size, output_dim, client, out):
                 dinv[4 + R * t + j] = di[:, j : j + 1]
                 blk[4 + R * t + j] = a_row[4 + R * t + j][:, col0 : col0 + K]
 
+        def rsqrt2(t, rest):
+            di = small.tile([P, R], F32, name="di")
+            last = R - 1
+            nc.scalar.activation(out=di[:, 0:last], in_=d[t][:, 0:last], func=ACT.Abs_reciprocal_sqrt, bias=1.0)
+            nc.scalar.activation(out=di[:, last:R], in_=d[t][:, last:R], func=ACT.Abs_reciprocal_sqrt, bias=rest)
+            for j in range(R):
+                dinv[4 + R * t + j] = di[:, j : j + 1]
+                blk[4 + R * t + j] = a_row[4 + R * t + j][:, col0 : col0 + K]
+
         def scale(n):
             q, j = divmod(n, 2)
             colb = work.tile([P, K], BF16, name="colb")
             if j == 0:
                 xt[q] = ps_t.tile([P, 2, 2, P], F32, name="xt")
             nc.vector.scalar_tensor_tensor(
-                out=colb[:], in0=blk[n], scalar=dinv[n], in1=dj_flat, op0=ALU.mult, op1=ALU.mult
+                out=colb[:].rearrange("m (n r) -> m n r", r=4),
+                in0=blk[n].rearrange("m (n r) -> m n r", r=4),
+                scalar=dinv[n],
+                in1=dj_flat,
+                op0=ALU.mult,
+                op1=ALU.mult,
             )
             words = colb[:].bitcast(F32)
             for w in range(2):
@@ -159,19 +203,15 @@ def tile_gcn_kernel(tc, adj, feats, batch_size, output_dim, client, out):
 
         def leave(n, engine):
             t, j = (-1, n) if n < 4 else divmod(n - 4, R)
-            rows = 4 if t < 0 else R
-            if j == 0:
-                y_sb[t] = ypool.tile([P, 2, rows, 256], F32, name="y_sb%d" % (t + 1))
-            engine(out=y_sb[t][:, :, j, :], in_=y_ps[n][:].rearrange("p (b f) -> p b f", b=2))
-            first = col0 if t < 0 else base[t]
+            first, rows, r0 = (col0, 4, 0) if t < 0 else place[t]
+            r = r0 + j
+            if r == 0:
+                y_sb[first] = ypool.tile([P, 2, rows, 256], F32, name="y_sb%d" % first)
+            engine(out=y_sb[first][:, :, r, :], in_=y_ps[n][:].rearrange("p (b f) -> p b f", b=2))
             dst = out[:, first : first + P * rows, :].rearrange("b (p r) f -> p b r f", r=rows)
-            if t == LAST:
-                stores.append((dst[:, :, j, :], y_sb[t][:, :, j, :]))
-            elif j == rows - 1:
-                stores.append((
-                    out[:, first : first + P * rows, :].rearrange("b (p r) f -> p b (r f)", r=rows),
-                    y_sb[t][:].rearrange("p b r f -> p b (r f)"),
-                ))
+            if r == rows - 1 or (t == LAST and j == 1):
+                lo = 0 if t != LAST or j == 1 else 2
+                stores.append((dst[:, :, lo : r + 1, :].rearrange("p b r f -> p b (r f)"), y_sb[first][:, :, lo : r + 1, :].rearrange("p b r f -> p b (r f)")))
 
         load_client(0, 4)
         nc.sync.dma_start(out=x_raw[:], in_=feats.rearrange("(q t) f -> q t f", t=4))
@@ -186,7 +226,6 @@ def tile_gcn_kernel(tc, adj, feats, batch_size, output_dim, client, out):
         nc.vector.memset(warm[:], 1.0)
         nc.scalar.activation(out=warm[:], in_=warm[:], func=ACT.Abs_reciprocal_sqrt)
 
-        dj_ps = ps_t.tile([P, 4, P], F32, name="xt")
         for r in range(4):
             client_row(r)
             nc.tensor.matmul(
@@ -197,7 +236,6 @@ def tile_gcn_kernel(tc, adj, feats, batch_size, output_dim, client, out):
                 stop=True,
             )
         nc.scalar.copy(out=x_grp[:], in_=x_raw[:].rearrange("q t f -> q f t"))
-        nc.vector.tensor_copy(out=djb[:], in_=dj_ps[:].rearrange("m r n -> m n r"))
         for n in range(4):
             scale(n)
         nc.vector.quantize_mx(
@@ -211,19 +249,25 @@ def tile_gcn_kernel(tc, adj, feats, batch_size, output_dim, client, out):
         left = 0
         for t in range(T - 1):
             ready = range(quanted, done // 2)
-            if t >= 1:
+            if t == 0:
+                sums_scalar(t)
+                for q in ready:
+                    regroup(q)
+                sums_vector(t, 1)
+                sums_vector(t, 2)
+                for q in ready:
+                    quant_mm(q)
+            else:
                 rsqrt(t - 1)
-            for q in ready:
-                regroup(q)
-            sums_scalar(t)
-            sums_vector(t, 1)
-            if t >= 1:
+                for q in ready:
+                    regroup(q)
+                sums_scalar(t)
+                sums_vector(t, 1)
                 scale(done)
                 scale(done + 1)
-            for q in ready:
-                quant_mm(q)
-            sums_vector(t, 2)
-            if t >= 1:
+                for q in ready:
+                    quant_mm(q)
+                sums_vector(t, 2)
                 scale(done + 2)
                 done += 3
             quanted = ready.stop
@@ -231,9 +275,9 @@ def tile_gcn_kernel(tc, adj, feats, batch_size, output_dim, client, out):
                 if loaded < T:
                     load(loaded)
                     loaded += 1
-            for n in range(left, 2 * quanted):
+            for n in range(left, 2 * quanted if t > 0 else 0):
                 leave(n, nc.scalar.copy)
-            left = 2 * quanted
+                left = n + 1
             if loaded == T:
                 for dst, src in stores:
                     nc.sync.dma_start(out=dst, in_=src)
@@ -242,21 +286,25 @@ def tile_gcn_kernel(tc, adj, feats, batch_size, output_dim, client, out):
         rsqrt(T - 2)
         regroup(9)
         regroup(10)
-        sums_scalar(T - 1)
-        sums_vector(T - 1, 1)
+        d[LAST] = small.tile([P, R], F32, name="d")
+        d2 = small.tile([P, 1], F32, name="d2")
+        sums_vector(LAST, 1)
+        presum_tensor(4 + R * LAST)
         quant_mm(9)
         quant_mm(10)
-        sums_vector(T - 1, 2)
-        rsqrt(T - 1)
+        sum_scalar(4 + R * LAST + 2, CT, d2[:], 1.0 / CT)
+        sum_vector(4 + R * LAST + 2, N - CT, d[LAST][:, 2:3])
+        sum_presummed(4 + R * LAST, d[LAST][:, 0:1])
+        leave(18, S)
+        rsqrt2(LAST, d2[:])
         scale(22)
         scale(23)
-        leave(18, S)
         leave(19, S)
+        leave(20, S)
+        leave(21, S)
         regroup(11)
         scale(24)
         scale(25)
-        leave(20, S)
-        leave(21, S)
         quant_mm(11)
         regroup(12)
         scale(26)

@@ -20,7 +20,7 @@ CS = 1152
 R = 3
 T = (N - K) // (P * R)
 UNITS = [(0, 12), (2048, 3), (2432, 3), (2816, 3), (3200, 3)]
-LUMPS = {t: [1, 1, 1] for t in range(8)}
+LUMPS = {t: [2, 1] for t in range(8)}
 A_BUFS = 6
 LAST = T - 1
 CT = 1536

@@ -19,7 +19,7 @@ K = 512
 CS = 1152
 R = 3
 T = (N - K) // (P * R)
-UNITS = [(0, 12), (2048, 3), (2432, 3), (2816, 3), (3200, 3)]
+UNITS = [(0, 12), (2048, 6), (2816, 3), (3200, 3)]
 LUMPS = {t: [2, 1] for t in range(8)}
 A_BUFS = 6
 LAST = T - 1
@@ -209,8 +209,8 @@ def tile_gcn_kernel(tc, adj, feats, batch_size, output_dim, client, out):
                 y_sb[first] = ypool.tile([P, 2, rows, 256], F32, name="y_sb%d" % first)
             engine(out=y_sb[first][:, :, r, :], in_=y_ps[n][:].rearrange("p (b f) -> p b f", b=2))
             dst = out[:, first : first + P * rows, :].rearrange("b (p r) f -> p b r f", r=rows)
-            if r == rows - 1 or (t == LAST and j == 1):
-                lo = 0 if t != LAST or j == 1 else 2
+            if r == rows - 1:
+                lo = 0
                 stores.append((dst[:, :, lo : r + 1, :].rearrange("p b r f -> p b (r f)"), y_sb[first][:, :, lo : r + 1, :].rearrange("p b r f -> p b (r f)")))
 
         load_client(0, 4)

@@ -53,7 +53,7 @@ def tile_gcn_kernel(tc, adj, feats, batch_size, output_dim, client, out):
         ident_b = const.tile([P, P], BF16, name="ident_b")
         ident_f = const.tile([P, P], F32, name="ident_f")
         epad = const.tile([P, K + 4], BF16, name="epad")
-        x_raw = const.tile([P, 4, K], BF16, name="x_raw")
+        x_raw = const.tile([P, 4, K], BF16, name="x_raw", align_bytes=256)
         x_grp = const.tile([P, K, 4], BF16, name="x_grp", align_bytes=64)
         x_codes = const.tile([P, K], U32, name="x_codes", align_bytes=64)
         x_scales = const.tile([P, K], U8, name="x_scales", align_bytes=64)
@@ -67,13 +67,13 @@ def tile_gcn_kernel(tc, adj, feats, batch_size, output_dim, client, out):
         def load_client(lo, hi):
             for t0 in range(lo, hi):
                 if t0 % R == 0:
-                    a_row["tile"] = apool.tile([P, R, N], BF16, name="a_t")
+                    a_row["tile"] = apool.tile([P, R, N], BF16, name="a_t", align_bytes=256)
                 a_row[t0] = a_row["tile"][:, t0 % R, :]
                 src = adj[col0 : col0 + K, :].rearrange("(p r) c -> p r c", r=4)
                 nc.sync.dma_start(out=a_row["tile"][:, t0 % R : t0 % R + 1, :], in_=src[:, t0 : t0 + 1, :])
 
         def load(t):
-            a_t = apool.tile([P, R, N], BF16, name="a_t")
+            a_t = apool.tile([P, R, N], BF16, name="a_t", align_bytes=256)
             first, width, r0 = place[t]
             src = adj[first : first + P * width, :].rearrange("(p r) c -> p r c", r=width)
             j = 0
@@ -206,7 +206,7 @@ def tile_gcn_kernel(tc, adj, feats, batch_size, output_dim, client, out):
             first, rows, r0 = (col0, 4, 0) if t < 0 else place[t]
             r = r0 + j
             if r == 0:
-                y_sb[first] = ypool.tile([P, 2, rows, 256], F32, name="y_sb%d" % first)
+                y_sb[first] = ypool.tile([P, 2, rows, 256], F32, name="y_sb%d" % first, align_bytes=256)
             engine(out=y_sb[first][:, :, r, :], in_=y_ps[n][:].rearrange("p (b f) -> p b f", b=2))
             dst = out[:, first : first + P * rows, :].rearrange("b (p r) f -> p b r f", r=rows)
             if r == rows - 1:

@@ -23,6 +23,8 @@ UNITS = [(0, 12), (2048, 6), (2816, 3), (3200, 3)]
 LUMPS = {t: [2, 1] for t in range(8)}
 A_BUFS = 6
 LAST = T - 1
+PRE = 4
+SH = 2048
 CT = 1536
 
 
@@ -47,7 +49,7 @@ def tile_gcn_kernel(tc, adj, feats, batch_size, output_dim, client, out):
         ps_y = ctx.enter_context(tc.psum_pool(name="ps_y", bufs=4))
         ctx.enter_context(tc.manual_schedule())
 
-        a_row, d, pre, dinv, blk = {}, {}, {}, {}, {}
+        a_row, rest, rest2, d, pre, dinv, blk = {}, {}, {}, {}, {}, {}, {}
         colb, xt, grp, codes, scl, y_ps, y_sb = {}, {}, {}, {}, {}, {}, {}
 
         ident_b = const.tile([P, P], BF16, name="ident_b")
@@ -96,8 +98,7 @@ def tile_gcn_kernel(tc, adj, feats, batch_size, output_dim, client, out):
                 accum_out=acc,
             )
 
-        def presum_tensor(n):
-            chunks = N // K - 1
+        def presum_tensor(n, chunks):
             pre[n] = ps_t.tile([P, K], F32, name="xt")
             for c in range(chunks):
                 nc.tensor.matmul(
@@ -108,11 +109,11 @@ def tile_gcn_kernel(tc, adj, feats, batch_size, output_dim, client, out):
                     stop=c == chunks - 1,
                 )
 
-        def sum_presummed(n, acc):
+        def sum_presummed(n, chunks, acc):
             junk_v = junk.tile([P, N // 2], BF16, name="junk_v")
             nc.vector.scalar_tensor_tensor(
                 out=junk_v[:, 0:K],
-                in0=a_row[n][:, N - K : N],
+                in0=a_row[n][:, chunks * K : (chunks + 1) * K],
                 scalar=1.0,
                 in1=pre[n][:],
                 op0=ALU.mult,
@@ -141,6 +142,13 @@ def tile_gcn_kernel(tc, adj, feats, batch_size, output_dim, client, out):
 
         def sums_scalar(t):
             d[t] = small.tile([P, R], F32, name="d")
+            if t == PRE:
+                rest[t] = small.tile([P, 1], F32, name="rest")
+                presum_tensor(4 + R * t, 4)
+                rest2[t] = small.tile([P, 1], F32, name="rest2")
+                sum_scalar(4 + R * t, N - 5 * K, rest[t][:], 1.0 / (N - 5 * K))
+                sum_scalar(4 + R * t + 2, SH, rest2[t][:], 1.0 / SH)
+                return
             sum_scalar(4 + R * t, N, d[t][:, 0:1], 0.0)
 
         def sums_vector(t, j):
@@ -148,7 +156,16 @@ def tile_gcn_kernel(tc, adj, feats, batch_size, output_dim, client, out):
 
         def rsqrt(t):
             di = small.tile([P, R], F32, name="di")
-            nc.scalar.activation(out=di[:], in_=d[t][:], func=ACT.Abs_reciprocal_sqrt, bias=1.0)
+            if t == PRE:
+                nc.scalar.activation(
+                    out=di[:, 0:1], in_=d[t][:, 0:1], func=ACT.Abs_reciprocal_sqrt, bias=rest[t][:]
+                )
+                nc.scalar.activation(out=di[:, 1:2], in_=d[t][:, 1:2], func=ACT.Abs_reciprocal_sqrt, bias=1.0)
+                nc.scalar.activation(
+                    out=di[:, 2:R], in_=d[t][:, 2:R], func=ACT.Abs_reciprocal_sqrt, bias=rest2[t][:]
+                )
+            else:
+                nc.scalar.activation(out=di[:], in_=d[t][:], func=ACT.Abs_reciprocal_sqrt, bias=1.0)
             for j in range(R):
                 dinv[4 + R * t + j] = di[:, j : j + 1]
                 blk[4 + R * t + j] = a_row[4 + R * t + j][:, col0 : col0 + K]
@@ -183,6 +200,35 @@ def tile_gcn_kernel(tc, adj, feats, batch_size, output_dim, client, out):
             grp[q] = work.tile([P, 2, P, 4], BF16, name="grp", align_bytes=64)
             nc.scalar.copy(out=grp[q][:].bitcast(F32), in_=xt[q][:].rearrange("q r w i -> q r i w"))
 
+        def regroup_row(q, j):
+            if j == 0:
+                grp[q] = work.tile([P, 2, P, 4], BF16, name="grp", align_bytes=64)
+            nc.scalar.copy(
+                out=grp[q][:, j, :, :].rearrange("q i t -> q (i t)").bitcast(F32).rearrange("q (i w) -> q i w", w=2),
+                in_=xt[q][:, j, :, :].rearrange("q w i -> q i w"),
+            )
+
+        def quant_mm_row(q, j):
+            if j == 0:
+                codes[q] = work.tile([P, 2 * P], U32, name="codes", align_bytes=64)
+                scl[q] = work.tile([P, 2 * P], U8, name="scl", align_bytes=64)
+            cols = slice(j * P, (j + 1) * P)
+            nc.vector.quantize_mx(
+                out=codes[q][:, cols].bitcast(FP8X4),
+                scales=scl[q][:, cols],
+                in_=grp[q][:, j, :, :].rearrange("q i t -> q (i t)"),
+            )
+            y_ps[2 * q + j] = ps_y.tile([P, K], F32, name="y_ps")
+            nc.tensor.matmul_mx(
+                out=y_ps[2 * q + j][:],
+                lhsT=codes[q][:, cols].bitcast(FP8X4),
+                lhsT_scale=scl[q][:, cols],
+                rhs=x_codes[:].bitcast(FP8X4),
+                rhs_scale=x_scales[:],
+                start=True,
+                stop=True,
+            )
+
         def quant_mm(q):
             codes[q] = work.tile([P, 2 * P], U32, name="codes", align_bytes=64)
             scl[q] = work.tile([P, 2 * P], U8, name="scl", align_bytes=64)
@@ -209,8 +255,8 @@ def tile_gcn_kernel(tc, adj, feats, batch_size, output_dim, client, out):
                 y_sb[first] = ypool.tile([P, 2, rows, 256], F32, name="y_sb%d" % first, align_bytes=256)
             engine(out=y_sb[first][:, :, r, :], in_=y_ps[n][:].rearrange("p (b f) -> p b f", b=2))
             dst = out[:, first : first + P * rows, :].rearrange("b (p r) f -> p b r f", r=rows)
-            if r == rows - 1:
-                lo = 0
+            if r == rows - 1 or (t == LAST and j == 1):
+                lo = 2 if t == LAST and j == 2 else 0
                 stores.append((dst[:, :, lo : r + 1, :].rearrange("p b r f -> p b (r f)"), y_sb[first][:, :, lo : r + 1, :].rearrange("p b r f -> p b (r f)")))
 
         load_client(0, 4)
@@ -267,7 +313,12 @@ def tile_gcn_kernel(tc, adj, feats, batch_size, output_dim, client, out):
                 scale(done + 1)
                 for q in ready:
                     quant_mm(q)
-                sums_vector(t, 2)
+                if t == PRE:
+                    sum_presummed(4 + R * t, 4, d[t][:, 0:1])
+                if t == PRE:
+                    sum_vector(4 + R * t + 2, N - SH, d[t][:, 2:3])
+                else:
+                    sums_vector(t, 2)
                 scale(done + 2)
                 done += 3
             quanted = ready.stop
@@ -289,12 +340,12 @@ def tile_gcn_kernel(tc, adj, feats, batch_size, output_dim, client, out):
         d[LAST] = small.tile([P, R], F32, name="d")
         d2 = small.tile([P, 1], F32, name="d2")
         sums_vector(LAST, 1)
-        presum_tensor(4 + R * LAST)
+        presum_tensor(4 + R * LAST, 6)
         quant_mm(9)
         quant_mm(10)
         sum_scalar(4 + R * LAST + 2, CT, d2[:], 1.0 / CT)
         sum_vector(4 + R * LAST + 2, N - CT, d[LAST][:, 2:3])
-        sum_presummed(4 + R * LAST, d[LAST][:, 0:1])
+        sum_presummed(4 + R * LAST, 6, d[LAST][:, 0:1])
         leave(18, S)
         rsqrt2(LAST, d2[:])
         scale(22)
@@ -311,10 +362,12 @@ def tile_gcn_kernel(tc, adj, feats, batch_size, output_dim, client, out):
         scale(27)
         leave(22, S)
         quant_mm(12)
-        regroup(13)
+        regroup_row(13, 0)
         leave(23, V)
+        quant_mm_row(13, 0)
+        regroup_row(13, 1)
+        quant_mm_row(13, 1)
         leave(24, S)
-        quant_mm(13)
         leave(25, V)
         leave(26, S)
         leave(27, V)

from contextlib import ExitStack

import concourse.mybir as mybir
from concourse.masks import make_identity

FLOPS = 2 * 3584 * 512 * 512

BF16 = mybir.dt.bfloat16
F32 = mybir.dt.float32
U32 = mybir.dt.uint32
U8 = mybir.dt.uint8
FP8X4 = mybir.dt.float8_e4m3fn_x4
ALU = mybir.AluOpType
ACT = mybir.ActivationFunctionType

P = 128
N = 3584
K = 512
CS = 1152
R = 3
T = (N - K) // (P * R)
UNITS = [(0, 12), (2048, 6), (2816, 3), (3200, 3)]
LUMPS = {t: [2, 1] for t in range(8)}
A_BUFS = 6
LAST = T - 1
PRE = 4
SH = 2048
CT = 1536


def tile_gcn_kernel(tc, adj, feats, batch_size, output_dim, client, out):
    nc = tc.nc
    col0 = client * K
    place = []
    for first, width in UNITS:
        for r0 in range(0, width, R):
            place.append((first, width, r0))

    with ExitStack() as ctx:
        const = ctx.enter_context(tc.tile_pool(name="const", bufs=1))
        apool = ctx.enter_context(tc.tile_pool(name="apool", bufs=A_BUFS))
        junk = ctx.enter_context(tc.tile_pool(name="junk", bufs=2))
        junk1 = ctx.enter_context(tc.tile_pool(name="junk1", bufs=1))
        work = ctx.enter_context(tc.tile_pool(name="work", bufs=4))
        small = ctx.enter_context(tc.tile_pool(name="small", bufs=4))
        ypool = ctx.enter_context(tc.tile_pool(name="ypool", bufs=1))
        ps_t = ctx.enter_context(tc.psum_pool(name="ps_t", bufs=3))
        ps_d = ctx.enter_context(tc.psum_pool(name="ps_d", bufs=1))
        ps_y = ctx.enter_context(tc.psum_pool(name="ps_y", bufs=4))
        ctx.enter_context(tc.manual_schedule())

        a_row, rest, rest2, d, pre, dinv, blk = {}, {}, {}, {}, {}, {}, {}
        colb, xt, grp, codes, scl, y_ps, y_sb = {}, {}, {}, {}, {}, {}, {}

        ident_b = const.tile([P, P], BF16, name="ident_b")
        ident_f = const.tile([P, P], F32, name="ident_f")
        epad = const.tile([P, K + 4], BF16, name="epad")
        x_raw = const.tile([P, 4, K], BF16, name="x_raw", align_bytes=256)
        x_grp = const.tile([P, K, 4], BF16, name="x_grp", align_bytes=64)
        x_codes = const.tile([P, K], U32, name="x_codes", align_bytes=64)
        x_scales = const.tile([P, K], U8, name="x_scales", align_bytes=64)
        dj_ps = ps_d.tile([P, 4, P], F32, name="dj_ps")
        dj_flat = dj_ps[:].rearrange("m r n -> m n r")
        s_v = const.tile([P, 4], F32, name="s_v")
        s_s = const.tile([P, 4], F32, name="s_s")
        dinv0 = const.tile([P, 4], F32, name="dinv0")
        warm = const.tile([P, 1], F32, name="warm")

        def load_client(lo, hi):
            for t0 in range(lo, hi):
                if t0 % R == 0:
                    a_row["tile"] = apool.tile([P, R, N], BF16, name="a_t", align_bytes=256)
                a_row[t0] = a_row["tile"][:, t0 % R, :]
                src = adj[col0 : col0 + K, :].rearrange("(p r) c -> p r c", r=4)
                nc.sync.dma_start(out=a_row["tile"][:, t0 % R : t0 % R + 1, :], in_=src[:, t0 : t0 + 1, :])

        def load(t):
            a_t = apool.tile([P, R, N], BF16, name="a_t", align_bytes=256)
            first, width, r0 = place[t]
            src = adj[first : first + P * width, :].rearrange("(p r) c -> p r c", r=width)
            j = 0
            for rows in LUMPS.get(t, [R]):
                nc.sync.dma_start(out=a_t[:, j : j + rows, :], in_=src[:, r0 + j : r0 + j + rows, :])
                j += rows
            for j in range(R):
                a_row[4 + R * t + j] = a_t[:, j, :]

        def sum_vector(n, cols, acc):
            half = cols // 2
            junk_v = junk.tile([P, N // 2], BF16, name="junk_v")
            nc.vector.scalar_tensor_tensor(
                out=junk_v[:, 0:half],
                in0=a_row[n][:, 0:half],
                scalar=1.0,
                in1=a_row[n][:, half : 2 * half],
                op0=ALU.mult,
                op1=ALU.add,
                accum_out=acc,
            )

        def presum_tensor(n, chunks):
            pre[n] = ps_t.tile([P, K], F32, name="xt")
            for c in range(chunks):
                nc.tensor.matmul(
                    out=pre[n][:],
                    lhsT=ident_b[:],
                    rhs=a_row[n][:, c * K : (c + 1) * K],
                    start=c == 0,
                    stop=c == chunks - 1,
                )

        def sum_presummed(n, chunks, acc):
            junk_v = junk.tile([P, N // 2], BF16, name="junk_v")
            nc.vector.scalar_tensor_tensor(
                out=junk_v[:, 0:K],
                in0=a_row[n][:, chunks * K : (chunks + 1) * K],
                scalar=1.0,
                in1=pre[n][:],
                op0=ALU.mult,
                op1=ALU.add,
                accum_out=acc,
            )

        def sum_scalar(n, cols, acc, bias):
            junk_s = junk1.tile([P, N], BF16, name="junk_s")
            nc.scalar.activation(
                out=junk_s[:, 0:cols], in_=a_row[n][:, N - cols : N], func=ACT.Copy, bias=bias, accum_out=acc
            )

        def client_row(r):
            sum_vector(r, N - CS, s_v[:, r : r + 1])
            sum_scalar(r, CS, s_s[:, r : r + 1], 1.0 / CS)
            nc.scalar.activation(
                out=dinv0[:, r : r + 1], in_=s_v[:, r : r + 1], func=ACT.Abs_reciprocal_sqrt, bias=s_s[:, r : r + 1]
            )
            dinv[r] = dinv0[:, r : r + 1]
            plus = const.tile([P, K], F32, name="plus%d" % r)
            nc.vector.tensor_tensor(
                out=plus[:], in0=a_row[r][:, col0 : col0 + K], in1=epad[:, 3 - r : 3 - r + K], op=ALU.add
            )
            blk[r] = plus[:]

        def sums_scalar(t):
            d[t] = small.tile([P, R], F32, name="d")
            if t == PRE:
                rest[t] = small.tile([P, 1], F32, name="rest")
                presum_tensor(4 + R * t, 4)
                rest2[t] = small.tile([P, 1], F32, name="rest2")
                sum_scalar(4 + R * t, N - 5 * K, rest[t][:], 1.0 / (N - 5 * K))
                sum_scalar(4 + R * t + 2, SH, rest2[t][:], 1.0 / SH)
                return
            sum_scalar(4 + R * t, N, d[t][:, 0:1], 0.0)

        def sums_vector(t, j):
            sum_vector(4 + R * t + j, N, d[t][:, j : j + 1])

        def rsqrt(t):
            di = small.tile([P, R], F32, name="di")
            if t == PRE:
                nc.scalar.activation(
                    out=di[:, 0:1], in_=d[t][:, 0:1], func=ACT.Abs_reciprocal_sqrt, bias=rest[t][:]
                )
                nc.scalar.activation(out=di[:, 1:2], in_=d[t][:, 1:2], func=ACT.Abs_reciprocal_sqrt, bias=1.0)
                nc.scalar.activation(
                    out=di[:, 2:R], in_=d[t][:, 2:R], func=ACT.Abs_reciprocal_sqrt, bias=rest2[t][:]
                )
            else:
                nc.scalar.activation(out=di[:], in_=d[t][:], func=ACT.Abs_reciprocal_sqrt, bias=1.0)
            for j in range(R):
                dinv[4 + R * t + j] = di[:, j : j + 1]
                blk[4 + R * t + j] = a_row[4 + R * t + j][:, col0 : col0 + K]

        def rsqrt2(t, rest):
            di = small.tile([P, R], F32, name="di")
            last = R - 1
            nc.scalar.activation(out=di[:, 0:last], in_=d[t][:, 0:last], func=ACT.Abs_reciprocal_sqrt, bias=1.0)
            nc.scalar.activation(out=di[:, last:R], in_=d[t][:, last:R], func=ACT.Abs_reciprocal_sqrt, bias=rest)
            for j in range(R):
                dinv[4 + R * t + j] = di[:, j : j + 1]
                blk[4 + R * t + j] = a_row[4 + R * t + j][:, col0 : col0 + K]

        def scale(n):
            q, j = divmod(n, 2)
            colb = work.tile([P, K], BF16, name="colb")
            if j == 0:
                xt[q] = ps_t.tile([P, 2, 2, P], F32, name="xt")
            nc.vector.scalar_tensor_tensor(
                out=colb[:].rearrange("m (n r) -> m n r", r=4),
                in0=blk[n].rearrange("m (n r) -> m n r", r=4),
                scalar=dinv[n],
                in1=dj_flat,
                op0=ALU.mult,
                op1=ALU.mult,
            )
            words = colb[:].bitcast(F32)
            for w in range(2):
                nc.tensor.transpose(xt[q][:, j, w, :], words[:, w : K // 2 : 2], ident_f[:])

        def regroup(q):
            grp[q] = work.tile([P, 2, P, 4], BF16, name="grp", align_bytes=64)
            nc.scalar.copy(out=grp[q][:].bitcast(F32), in_=xt[q][:].rearrange("q r w i -> q r i w"))

        def regroup_row(q, j):
            if j == 0:
                grp[q] = work.tile([P, 2, P, 4], BF16, name="grp", align_bytes=64)
            nc.scalar.copy(
                out=grp[q][:, j, :, :].rearrange("q i t -> q (i t)").bitcast(F32).rearrange("q (i w) -> q i w", w=2),
                in_=xt[q][:, j, :, :].rearrange("q w i -> q i w"),
            )

        def quant_mm_row(q, j):
            if j == 0:
                codes[q] = work.tile([P, 2 * P], U32, name="codes", align_bytes=64)
                scl[q] = work.tile([P, 2 * P], U8, name="scl", align_bytes=64)
            cols = slice(j * P, (j + 1) * P)
            nc.vector.quantize_mx(
                out=codes[q][:, cols].bitcast(FP8X4),
                scales=scl[q][:, cols],
                in_=grp[q][:, j, :, :].rearrange("q i t -> q (i t)"),
            )
            y_ps[2 * q + j] = ps_y.tile([P, K], F32, name="y_ps")
            nc.tensor.matmul_mx(
                out=y_ps[2 * q + j][:],
                lhsT=codes[q][:, cols].bitcast(FP8X4),
                lhsT_scale=scl[q][:, cols],
                rhs=x_codes[:].bitcast(FP8X4),
                rhs_scale=x_scales[:],
                start=True,
                stop=True,
            )

        def quant_mm(q):
            codes[q] = work.tile([P, 2 * P], U32, name="codes", align_bytes=64)
            scl[q] = work.tile([P, 2 * P], U8, name="scl", align_bytes=64)
            nc.vector.quantize_mx(
                out=codes[q][:].bitcast(FP8X4), scales=scl[q][:], in_=grp[q][:].rearrange("q r i t -> q (r i t)")
            )
            for j in range(2):
                y_ps[2 * q + j] = ps_y.tile([P, K], F32, name="y_ps")
                nc.tensor.matmul_mx(
                    out=y_ps[2 * q + j][:],
                    lhsT=codes[q][:, j * P : (j + 1) * P].bitcast(FP8X4),
                    lhsT_scale=scl[q][:, j * P : (j + 1) * P],
                    rhs=x_codes[:].bitcast(FP8X4),
                    rhs_scale=x_scales[:],
                    start=True,
                    stop=True,
                )

        def leave(n, engine):
            t, j = (-1, n) if n < 4 else divmod(n - 4, R)
            first, rows, r0 = (col0, 4, 0) if t < 0 else place[t]
            r = r0 + j
            if r == 0:
                y_sb[first] = ypool.tile([P, 2, rows, 256], F32, name="y_sb%d" % first, align_bytes=256)
            engine(out=y_sb[first][:, :, r, :], in_=y_ps[n][:].rearrange("p (b f) -> p b f", b=2))
            dst = out[:, first : first + P * rows, :].rearrange("b (p r) f -> p b r f", r=rows)
            if r == rows - 1 or (t == LAST and j == 1):
                lo = 2 if t == LAST and j == 2 else 0
                stores.append((dst[:, :, lo : r + 1, :].rearrange("p b r f -> p b (r f)"), y_sb[first][:, :, lo : r + 1, :].rearrange("p b r f -> p b (r f)")))

        load_client(0, 4)
        nc.sync.dma_start(out=x_raw[:], in_=feats.rearrange("(q t) f -> q t f", t=4))
        for t in range(A_BUFS - 2):
            load(t)
        make_identity(nc, ident_b[:])
        nc.gpsimd.memset(epad[:], 0.0)
        nc.gpsimd.tensor_copy(
            out=epad[:, 3 : 3 + K].rearrange("p (q r) -> p q r", r=4)[:, :, 0], in_=ident_b[:]
        )
        make_identity(nc, ident_f[:])
        nc.vector.memset(warm[:], 1.0)
        nc.scalar.activation(out=warm[:], in_=warm[:], func=ACT.Abs_reciprocal_sqrt)

        for r in range(4):
            client_row(r)
            nc.tensor.matmul(
                out=dj_ps[:, r, :],
                lhsT=dinv0[:, r : r + 1].to_broadcast([P, P]),
                rhs=ident_f[:],
                start=True,
                stop=True,
            )
        nc.scalar.copy(out=x_grp[:], in_=x_raw[:].rearrange("q t f -> q f t"))
        for n in range(4):
            scale(n)
        nc.vector.quantize_mx(
            out=x_codes[:].bitcast(FP8X4), scales=x_scales[:], in_=x_grp[:].rearrange("q f t -> q (f t)")
        )

        stores = []
        loaded = A_BUFS - 2
        done = 4
        quanted = 0
        left = 0
        for t in range(T - 1):
            ready = range(quanted, done // 2)
            if t == 0:
                sums_scalar(t)
                for q in ready:
                    regroup(q)
                sums_vector(t, 1)
                sums_vector(t, 2)
                for q in ready:
                    quant_mm(q)
            else:
                rsqrt(t - 1)
                for q in ready:
                    regroup(q)
                sums_scalar(t)
                sums_vector(t, 1)
                scale(done)
                scale(done + 1)
                for q in ready:
                    quant_mm(q)
                if t == PRE:
                    sum_presummed(4 + R * t, 4, d[t][:, 0:1])
                if t == PRE:
                    sum_vector(4 + R * t + 2, N - SH, d[t][:, 2:3])
                else:
                    sums_vector(t, 2)
                scale(done + 2)
                done += 3
            quanted = ready.stop
            for step in range(2 if t == 0 else 1):
                if loaded < T:
                    load(loaded)
                    loaded += 1
            for n in range(left, 2 * quanted if t > 0 else 0):
                leave(n, nc.scalar.copy)
                left = n + 1
            if loaded == T:
                for dst, src in stores:
                    nc.sync.dma_start(out=dst, in_=src)
                stores = []
        V, S = nc.vector.tensor_copy, nc.scalar.copy
        rsqrt(T - 2)
        regroup(9)
        regroup(10)
        d[LAST] = small.tile([P, R], F32, name="d")
        d2 = small.tile([P, 1], F32, name="d2")
        sums_vector(LAST, 1)
        presum_tensor(4 + R * LAST, 6)
        quant_mm(9)
        quant_mm(10)
        sum_scalar(4 + R * LAST + 2, CT, d2[:], 1.0 / CT)
        sum_vector(4 + R * LAST + 2, N - CT, d[LAST][:, 2:3])
        sum_presummed(4 + R * LAST, 6, d[LAST][:, 0:1])
        leave(18, S)
        rsqrt2(LAST, d2[:])
        scale(22)
        scale(23)
        leave(19, S)
        leave(20, S)
        leave(21, S)
        regroup(11)
        scale(24)
        scale(25)
        quant_mm(11)
        regroup(12)
        scale(26)
        scale(27)
        leave(22, S)
        quant_mm(12)
        regroup_row(13, 0)
        leave(23, V)
        quant_mm_row(13, 0)
        regroup_row(13, 1)
        quant_mm_row(13, 1)
        leave(24, S)
        leave(25, V)
        leave(26, S)
        leave(27, V)
        for dst, src in stores:
            nc.sync.dma_start(out=dst, in_=src)
